import numpy as np
import ml_dtypes


def mxq(x, axis, fmt="e4m3"):
    dtype, down = {"e4m3": (ml_dtypes.float8_e4m3fn, 7), "e5m2": (ml_dtypes.float8_e5m2, 14)}[fmt]
    v = np.moveaxis(np.asarray(x, np.float32).astype(ml_dtypes.bfloat16).astype(np.float64), axis, -1)
    blocks = v.reshape(v.shape[:-1] + (-1, 32))
    amax = np.abs(blocks).max(-1, keepdims=True)
    byte = np.maximum(np.where(amax > 0, np.frexp(amax)[1] - 1 + 127, 0) - down, 1)
    scale = np.exp2(byte - 127.0)
    codes = (blocks / scale).astype(np.float32).astype(dtype).astype(np.float64)
    return np.moveaxis((codes * scale).reshape(v.shape), -1, axis)


WIDE = False


def mx_kscale(k):
    if not WIDE:
        return np.ones(k)
    levels = np.array([10, -10, 5, -5, 0])
    a = np.random.permutation(np.resize(levels, k // 512 * 4)).reshape(k // 512, 4)
    idx = np.arange(k)
    return np.exp2(a[idx // 512, idx % 128 // 32])


BF16 = ml_dtypes.bfloat16


def bf(x):
    return np.asarray(x, np.float32).astype(BF16)


def f64(x):
    return np.asarray(x).astype(np.float64)


B, N, IN_DIM, OUT_DIM, H = 8, 1024, 512, 256, 2
HEAD_DIM = OUT_DIM // H
EDGE_P = 0.01


def setup_inputs():
    s = mx_kscale(IN_DIM)
    adj = np.maximum((np.random.random((N, N)) < EDGE_P) * 1.0, np.eye(N))
    return {"q": bf(np.random.standard_normal((B, H, N, HEAD_DIM))),
            "k": bf(np.random.standard_normal((B, H, N, HEAD_DIM))),
            "h": bf(np.random.standard_normal((B, N, IN_DIM)) * s),
            "w_v": bf(np.random.standard_normal((IN_DIM, OUT_DIM)) / np.sqrt(IN_DIM) / s[:, None]),
            "adj": bf(adj)}


def reference(q, k, h, w_v, adj):
    v = mxq(f64(h), 2, "e4m3") @ mxq(f64(w_v), 0, "e4m3")
    v = v.reshape(B, N, H, HEAD_DIM).transpose(0, 2, 1, 3)
    mask = np.where(f64(adj) == 0, -np.inf, 0.0)
    s = f64(q) @ f64(k).transpose(0, 1, 3, 2) / np.sqrt(HEAD_DIM) + mask
    e = np.exp(s - s.max(-1, keepdims=True))
    out = (mxq(e, 3, "e4m3") @ mxq(v, 2, "e4m3")) / e.sum(-1, keepdims=True)
    return out.transpose(0, 2, 1, 3).reshape(B, N, OUT_DIM)

@@ -1,0 +1,225 @@
+import math
+from contextlib import ExitStack
+
+import concourse.mybir as mybir
+from concourse.masks import make_identity
+
+F32 = mybir.dt.float32
+BF16 = mybir.dt.bfloat16
+U32 = mybir.dt.uint32
+U8 = mybir.dt.uint8
+FP8X4 = mybir.dt.float8_e4m3fn_x4
+ALU = mybir.AluOpType
+FUNC = mybir.ActivationFunctionType
+
+BATCH = 8
+HEADS = 2
+NODES = 1024
+HEAD_DIM = 128
+IN_DIM = 512
+
+P = 128
+PACK = 4
+PAIR = 2
+K_PASS = P * PACK
+BANK = 512
+ROW_TILES = NODES // P
+NODE_PASSES = NODES // K_PASS
+NODE_TILES = NODE_PASSES * PACK
+SCALE = 1.0 / math.sqrt(HEAD_DIM)
+MASKED = 1.0e30
+
+FLOPS = 2 * BATCH * NODES * IN_DIM * HEADS * HEAD_DIM + 2 * 2 * BATCH * HEADS * NODES * NODES * HEAD_DIM
+
+
+def block(index, width):
+    return slice(index * width, (index + 1) * width)
+
+
+def tile_gatlayer_pa_t_kernel(tc, q, k, h, w_v, adj, out):
+    nc = tc.nc
+    with ExitStack() as stack:
+        const = stack.enter_context(tc.tile_pool(name="const", bufs=1))
+        batch = stack.enter_context(tc.tile_pool(name="batch", bufs=2))
+        work = stack.enter_context(tc.tile_pool(name="work", bufs=3))
+        psum_s = stack.enter_context(tc.psum_pool(name="psum_s", bufs=4))
+        psum_e = stack.enter_context(tc.psum_pool(name="psum_e", bufs=2))
+        psum_o = stack.enter_context(tc.psum_pool(name="psum_o", bufs=1))
+        psum_b = stack.enter_context(tc.psum_pool(name="psum_b", bufs=1))
+
+        ident_bf16 = const.tile([P, P], BF16)
+        make_identity(nc, ident_bf16[:])
+        ident_f32 = const.tile([P, P], F32)
+        make_identity(nc, ident_f32[:])
+
+        def load_batch(b):
+            q_rows = batch.tile([P, HEADS, ROW_TILES, HEAD_DIM], BF16)
+            nc.sync.dma_start(out=q_rows[:], in_=q[b].rearrange("n (t p) d -> p n t d", p=P))
+            k_rows = batch.tile([P, HEADS, ROW_TILES, HEAD_DIM], BF16)
+            nc.sync.dma_start(out=k_rows[:], in_=k[b].rearrange("n (t p) d -> p n t d", p=P))
+            h_rows = batch.tile([P, NODE_TILES // PAIR, PAIR, IN_DIM], BF16)
+            nc.sync.dma_start(out=h_rows[:], in_=h[b].rearrange("(c p e) f -> p c e f", p=P, e=PAIR))
+            return q_rows, k_rows, h_rows
+
+        def prepare_batch(q_rows, k_rows, h_rows):
+            q_cols = batch.tile([P, HEADS, NODES], BF16)
+            k_cols = batch.tile([P, HEADS, NODES], BF16)
+            for rows, cols in ((q_rows, q_cols), (k_rows, k_cols)):
+                for n in range(HEADS):
+                    flipped = psum_b.tile([P, ROW_TILES, P], BF16, name="flipped", tag="prepare")
+                    for t in range(ROW_TILES):
+                        nc.tensor.transpose(flipped[:, t, :], rows[:, n, t, :], ident_bf16[:])
+                    nc.scalar.copy(out=cols[:, n, :], in_=flipped[:].rearrange("p t i -> p (t i)"))
+
+            h_words = h_rows[:].bitcast(F32)
+            h_grouped = batch.tile([P, NODE_TILES, P, PACK], BF16, align_bytes=64)
+            h_grouped_words = h_grouped[:].bitcast(F32)
+            for c in range(NODE_TILES // PAIR):
+                h_flipped = psum_b.tile([P, PAIR, PAIR, P], F32, name="h_flipped", tag="prepare")
+                for e in range(PAIR):
+                    for u in range(PAIR):
+                        nc.tensor.transpose(h_flipped[:, e, u, :], h_words[:, c, e, block(u, P)], ident_f32[:])
+                nc.scalar.copy(
+                    out=h_grouped_words[:, block(c, PAIR), :, :],
+                    in_=h_flipped[:].rearrange("p e u r -> p e r u"),
+                )
+            h_codes = batch.tile([P, NODES], U32, align_bytes=64)
+            h_scales = batch.tile([P, NODES], U8, align_bytes=64)
+            nc.vector.quantize_mx(
+                out=h_codes[:].bitcast(FP8X4),
+                scales=h_scales[:],
+                in_=h_grouped[:].rearrange("p s r t -> p (s r t)"),
+            )
+
+            v_grouped = batch.tile([P, NODE_PASSES, HEADS, HEAD_DIM, PACK], BF16, align_bytes=64)
+            for g in range(NODE_PASSES):
+                for n in range(HEADS):
+                    v_sums = psum_b.tile([P, PACK, HEAD_DIM], F32, name="v_sums", tag="prepare")
+                    for t in range(PACK):
+                        nc.tensor.matmul_mx(
+                            out=v_sums[:, t, :],
+                            lhsT=h_codes[:, block(PACK * g + t, P)].bitcast(FP8X4),
+                            lhsT_scale=h_scales[:, block(PACK * g + t, P)],
+                            rhs=w_codes[:, block(n, HEAD_DIM)].bitcast(FP8X4),
+                            rhs_scale=w_scales[:, block(n, HEAD_DIM)],
+                            start=True,
+                            stop=True,
+                        )
+                    nc.scalar.copy(out=v_grouped[:, g, n, :, :], in_=v_sums[:].rearrange("p t d -> p d t"))
+            v_codes = batch.tile([P, NODE_PASSES * HEADS * HEAD_DIM], U32, align_bytes=64)
+            v_scales = batch.tile([P, NODE_PASSES * HEADS * HEAD_DIM], U8, align_bytes=64)
+            nc.vector.quantize_mx(
+                out=v_codes[:].bitcast(FP8X4),
+                scales=v_scales[:],
+                in_=v_grouped[:].rearrange("p g n d t -> p (g n d t)"),
+            )
+            return q_cols, k_cols, v_codes, v_scales
+
+        def attend(b, it, q_cols, k_cols, v_codes, v_scales):
+            scores = work.tile([P, HEADS, NODES], F32)
+            for n in range(HEADS):
+                for half in range(NODES // BANK):
+                    s_sums = psum_s.tile([P, BANK], F32)
+                    nc.tensor.matmul(
+                        out=s_sums[:],
+                        lhsT=q_cols[:, n, block(it, P)],
+                        rhs=k_cols[:, n, block(half, BANK)],
+                        start=True,
+                        stop=True,
+                    )
+                    nc.vector.scalar_tensor_tensor(
+                        out=scores[:, n, block(half, BANK)],
+                        in0=s_sums[:],
+                        scalar=SCALE,
+                        in1=mask_bias[:, it, block(half, BANK)],
+                        op0=ALU.mult,
+                        op1=ALU.add,
+                    )
+            neg_max = work.tile([P, HEADS], F32)
+            nc.vector.tensor_reduce(out=neg_max[:], in_=scores[:], axis=mybir.AxisListType.X, op=ALU.max, negate=True)
+
+            e_rows = work.tile([P, HEADS, NODES], BF16)
+            row_sum = work.tile([P, HEADS], F32)
+            for n in range(HEADS):
+                nc.scalar.activation(
+                    out=e_rows[:, n, :],
+                    in_=scores[:, n, :],
+                    func=FUNC.Exp,
+                    bias=neg_max[:, n : n + 1],
+                    scale=1.0,
+                    accum_out=row_sum[:, n : n + 1],
+                )
+
+            e_words = e_rows[:].bitcast(F32)
+            e_grouped = work.tile([P, HEADS, NODE_PASSES, P, PACK], BF16, align_bytes=64)
+            e_grouped_words = e_grouped[:].bitcast(F32)
+            for n in range(HEADS):
+                e_flipped = psum_e.tile([P, NODE_PASSES, PAIR, P], F32)
+                for g in range(NODE_PASSES):
+                    for u in range(PAIR):
+                        nc.tensor.transpose(e_flipped[:, g, u, :], e_words[:, n, block(PAIR * g + u, P)], ident_f32[:])
+                nc.scalar.copy(out=e_grouped_words[:, n], in_=e_flipped[:].rearrange("p g u i -> p g i u"))
+            e_codes = work.tile([P, HEADS * NODE_PASSES * P], U32, align_bytes=64)
+            e_scales = work.tile([P, HEADS * NODE_PASSES * P], U8, align_bytes=64)
+            nc.vector.quantize_mx(
+                out=e_codes[:].bitcast(FP8X4),
+                scales=e_scales[:],
+                in_=e_grouped[:].rearrange("p n g i t -> p (n g i t)"),
+            )
+
+            o_sums = psum_o.tile([P, HEADS, HEAD_DIM], F32)
+            for n in range(HEADS):
+                for g in range(NODE_PASSES):
+                    nc.tensor.matmul_mx(
+                        out=o_sums[:, n, :],
+                        lhsT=e_codes[:, block(NODE_PASSES * n + g, P)].bitcast(FP8X4),
+                        lhsT_scale=e_scales[:, block(NODE_PASSES * n + g, P)],
+                        rhs=v_codes[:, block(HEADS * g + n, HEAD_DIM)].bitcast(FP8X4),
+                        rhs_scale=v_scales[:, block(HEADS * g + n, HEAD_DIM)],
+                        start=(g == 0),
+                        stop=(g == NODE_PASSES - 1),
+                    )
+            inv_sum = work.tile([P, HEADS], F32)
+            nc.vector.reciprocal(out=inv_sum[:], in_=row_sum[:])
+            o_rows = work.tile([P, HEADS, HEAD_DIM], F32)
+            for n in range(HEADS):
+                nc.scalar.activation(out=o_rows[:, n, :], in_=o_sums[:, n, :], func=FUNC.Copy, scale=inv_sum[:, n : n + 1])
+            nc.gpsimd.dma_start(out=out[b, block(it, P), :], in_=o_rows[:].rearrange("p n d -> p (n d)"))
+
+        loaded = load_batch(0)
+
+        w_rows = const.tile([P, PACK, HEADS * HEAD_DIM], BF16)
+        for u in range(PAIR):
+            nc.sync.dma_start(
+                out=w_rows[:, block(u, PAIR), :],
+                in_=w_v[block(u, PAIR * P), :].rearrange("(p e) c -> p e c", e=PAIR),
+            )
+        w_grouped = const.tile([P, HEADS * HEAD_DIM, PACK], BF16, align_bytes=64)
+        nc.vector.tensor_copy(out=w_grouped[:], in_=w_rows[:].rearrange("p t c -> p c t"))
+        w_codes = const.tile([P, HEADS * HEAD_DIM], U32, align_bytes=64)
+        w_scales = const.tile([P, HEADS * HEAD_DIM], U8, align_bytes=64)
+        nc.vector.quantize_mx(
+            out=w_codes[:].bitcast(FP8X4),
+            scales=w_scales[:],
+            in_=w_grouped[:].rearrange("p c t -> p (c t)"),
+        )
+
+        mask_bias = const.tile([P, ROW_TILES, NODES], BF16)
+        for it in range(ROW_TILES):
+            nc.sync.dma_start(out=mask_bias[:, it, :], in_=adj[block(it, P), :])
+            nc.vector.tensor_scalar(
+                out=mask_bias[:, it, :],
+                in0=mask_bias[:, it, :],
+                scalar1=1.0,
+                scalar2=MASKED,
+                op0=ALU.subtract,
+                op1=ALU.mult,
+            )
+
+        prepared = prepare_batch(*loaded)
+        for b in range(BATCH):
+            current = prepared
+            if b + 1 < BATCH:
+                prepared = prepare_batch(*load_batch(b + 1))
+            for it in range(ROW_TILES):
+                attend(b, it, *current)

@@ -23,6 +23,7 @@ PACK = 4
 PAIR = 2
 K_PASS = P * PACK
 BANK = 512
+HALVES = NODES // BANK
 ROW_TILES = NODES // P
 NODE_PASSES = NODES // K_PASS
 NODE_TILES = NODE_PASSES * PACK
@@ -42,10 +43,8 @@ def tile_gatlayer_pa_t_kernel(tc, q, k, h, w_v, adj, out):
         const = stack.enter_context(tc.tile_pool(name="const", bufs=1))
         batch = stack.enter_context(tc.tile_pool(name="batch", bufs=2))
         work = stack.enter_context(tc.tile_pool(name="work", bufs=3))
-        psum_s = stack.enter_context(tc.psum_pool(name="psum_s", bufs=4))
-        psum_e = stack.enter_context(tc.psum_pool(name="psum_e", bufs=2))
-        psum_o = stack.enter_context(tc.psum_pool(name="psum_o", bufs=1))
-        psum_b = stack.enter_context(tc.psum_pool(name="psum_b", bufs=1))
+        psum_s = stack.enter_context(tc.psum_pool(name="psum_s", bufs=5))
+        psum_x = stack.enter_context(tc.psum_pool(name="psum_x", bufs=3))
 
         ident_bf16 = const.tile([P, P], BF16)
         make_identity(nc, ident_bf16[:])
@@ -66,7 +65,7 @@ def tile_gatlayer_pa_t_kernel(tc, q, k, h, w_v, adj, out):
             k_cols = batch.tile([P, HEADS, NODES], BF16)
             for rows, cols in ((q_rows, q_cols), (k_rows, k_cols)):
                 for n in range(HEADS):
-                    flipped = psum_b.tile([P, ROW_TILES, P], BF16, name="flipped", tag="prepare")
+                    flipped = psum_x.tile([P, ROW_TILES, P], BF16, name="flipped", tag="shared")
                     for t in range(ROW_TILES):
                         nc.tensor.transpose(flipped[:, t, :], rows[:, n, t, :], ident_bf16[:])
                     nc.scalar.copy(out=cols[:, n, :], in_=flipped[:].rearrange("p t i -> p (t i)"))
@@ -75,7 +74,7 @@ def tile_gatlayer_pa_t_kernel(tc, q, k, h, w_v, adj, out):
             h_grouped = batch.tile([P, NODE_TILES, P, PACK], BF16, align_bytes=64)
             h_grouped_words = h_grouped[:].bitcast(F32)
             for c in range(NODE_TILES // PAIR):
-                h_flipped = psum_b.tile([P, PAIR, PAIR, P], F32, name="h_flipped", tag="prepare")
+                h_flipped = psum_x.tile([P, PAIR, PAIR, P], F32, name="h_flipped", tag="shared")
                 for e in range(PAIR):
                     for u in range(PAIR):
                         nc.tensor.transpose(h_flipped[:, e, u, :], h_words[:, c, e, block(u, P)], ident_f32[:])
@@ -94,7 +93,7 @@ def tile_gatlayer_pa_t_kernel(tc, q, k, h, w_v, adj, out):
             v_grouped = batch.tile([P, NODE_PASSES, HEADS, HEAD_DIM, PACK], BF16, align_bytes=64)
             for g in range(NODE_PASSES):
                 for n in range(HEADS):
-                    v_sums = psum_b.tile([P, PACK, HEAD_DIM], F32, name="v_sums", tag="prepare")
+                    v_sums = psum_x.tile([P, PACK, HEAD_DIM], F32, name="v_sums", tag="shared")
                     for t in range(PACK):
                         nc.tensor.matmul_mx(
                             out=v_sums[:, t, :],
@@ -116,49 +115,64 @@ def tile_gatlayer_pa_t_kernel(tc, q, k, h, w_v, adj, out):
             return q_cols, k_cols, v_codes, v_scales
 
         def attend(b, it, q_cols, k_cols, v_codes, v_scales):
-            scores = work.tile([P, HEADS, NODES], F32)
+            e_rows = work.tile([P, HEADS, NODES], BF16)
+            e_words = e_rows[:].bitcast(F32)
+            e_grouped = work.tile([P, HEADS, NODE_PASSES, P, PACK], BF16, align_bytes=64)
+            e_grouped_words = e_grouped[:].bitcast(F32)
+            part_sum = work.tile([P, HEADS, HALVES], F32)
             for n in range(HEADS):
-                for half in range(NODES // BANK):
+                banks = []
+                part_max = work.tile([P, HALVES], F32)
+                for half in range(HALVES):
                     s_sums = psum_s.tile([P, BANK], F32)
                     nc.tensor.matmul(
                         out=s_sums[:],
                         lhsT=q_cols[:, n, block(it, P)],
                         rhs=k_cols[:, n, block(half, BANK)],
                         start=True,
-                        stop=True,
+                        stop=False,
                     )
-                    nc.vector.scalar_tensor_tensor(
-                        out=scores[:, n, block(half, BANK)],
-                        in0=s_sums[:],
-                        scalar=SCALE,
-                        in1=mask_bias[:, it, block(half, BANK)],
-                        op0=ALU.mult,
-                        op1=ALU.add,
+                    for c in range(BANK // P):
+                        nc.tensor.matmul(
+                            out=s_sums[:, block(c, P)],
+                            lhsT=mask_cols[:, it, (BANK // P) * half + c, :],
+                            rhs=ident_f32[:],
+                            is_transpose=True,
+                            start=False,
+                            stop=(c == BANK // P - 1),
+                        )
+                    nc.vector.tensor_reduce(
+                        out=part_max[:, half : half + 1], in_=s_sums[:], axis=mybir.AxisListType.X, op=ALU.max
                     )
-            neg_max = work.tile([P, HEADS], F32)
-            nc.vector.tensor_reduce(out=neg_max[:], in_=scores[:], axis=mybir.AxisListType.X, op=ALU.max, negate=True)
-
-            e_rows = work.tile([P, HEADS, NODES], BF16)
-            row_sum = work.tile([P, HEADS], F32)
-            for n in range(HEADS):
-                nc.scalar.activation(
-                    out=e_rows[:, n, :],
-                    in_=scores[:, n, :],
-                    func=FUNC.Exp,
-                    bias=neg_max[:, n : n + 1],
-                    scale=1.0,
-                    accum_out=row_sum[:, n : n + 1],
+                    banks.append(s_sums)
+                neg_max = work.tile([P, 1], F32)
+                nc.vector.tensor_scalar(
+                    out=neg_max[:],
+                    in0=part_max[:, 0:1],
+                    scalar1=part_max[:, 1:2],
+                    scalar2=-SCALE,
+                    op0=ALU.max,
+                    op1=ALU.mult,
                 )
-
-            e_words = e_rows[:].bitcast(F32)
-            e_grouped = work.tile([P, HEADS, NODE_PASSES, P, PACK], BF16, align_bytes=64)
-            e_grouped_words = e_grouped[:].bitcast(F32)
-            for n in range(HEADS):
-                e_flipped = psum_e.tile([P, NODE_PASSES, PAIR, P], F32)
+                for half in range(HALVES):
+                    nc.scalar.activation(
+                        out=e_rows[:, n, block(half, BANK)],
+                        in_=banks[half][:],
+                        func=FUNC.Exp,
+                        bias=neg_max[:],
+                        scale=SCALE,
+                        accum_out=part_sum[:, n, half : half + 1],
+                    )
+                e_flipped = psum_x.tile([P, NODE_PASSES, PAIR, P], F32, name="e_flipped", tag="shared")
                 for g in range(NODE_PASSES):
                     for u in range(PAIR):
                         nc.tensor.transpose(e_flipped[:, g, u, :], e_words[:, n, block(PAIR * g + u, P)], ident_f32[:])
-                nc.scalar.copy(out=e_grouped_words[:, n], in_=e_flipped[:].rearrange("p g u i -> p g i u"))
+                if n == 0:
+                    nc.scalar.copy(out=e_grouped_words[:, n], in_=e_flipped[:].rearrange("p g u i -> p g i u"))
+                else:
+                    nc.vector.tensor_copy(out=e_grouped_words[:, n], in_=e_flipped[:].rearrange("p g u i -> p g i u"))
+            row_sum = work.tile([P, HEADS], F32)
+            nc.vector.tensor_reduce(out=row_sum[:], in_=part_sum[:], axis=mybir.AxisListType.X, op=ALU.add)
             e_codes = work.tile([P, HEADS * NODE_PASSES * P], U32, align_bytes=64)
             e_scales = work.tile([P, HEADS * NODE_PASSES * P], U8, align_bytes=64)
             nc.vector.quantize_mx(
@@ -167,7 +181,7 @@ def tile_gatlayer_pa_t_kernel(tc, q, k, h, w_v, adj, out):
                 in_=e_grouped[:].rearrange("p n g i t -> p (n g i t)"),
             )
 
-            o_sums = psum_o.tile([P, HEADS, HEAD_DIM], F32)
+            o_sums = psum_x.tile([P, HEADS, HEAD_DIM], F32, name="o_sums", tag="shared")
             for n in range(HEADS):
                 for g in range(NODE_PASSES):
                     nc.tensor.matmul_mx(
@@ -204,12 +218,16 @@ def tile_gatlayer_pa_t_kernel(tc, q, k, h, w_v, adj, out):
             in_=w_grouped[:].rearrange("p c t -> p (c t)"),
         )
 
-        mask_bias = const.tile([P, ROW_TILES, NODES], BF16)
+        adj_rows = const.tile([P, ROW_TILES, NODES], BF16)
+        mask_cols = const.tile([P, ROW_TILES, NODES // P, P], F32)
         for it in range(ROW_TILES):
-            nc.sync.dma_start(out=mask_bias[:, it, :], in_=adj[block(it, P), :])
+            nc.sync.dma_start(out=adj_rows[:, it, :], in_=adj[block(it, P), :])
+            adj_flipped = psum_x.tile([P, NODES // P, P], BF16, name="adj_flipped", tag="shared")
+            for c in range(NODES // P):
+                nc.tensor.transpose(adj_flipped[:, c, :], adj_rows[:, it, block(c, P)], ident_bf16[:])
             nc.vector.tensor_scalar(
-                out=mask_bias[:, it, :],
-                in0=mask_bias[:, it, :],
+                out=mask_cols[:, it, :, :],
+                in0=adj_flipped[:],
                 scalar1=1.0,
                 scalar2=MASKED,
                 op0=ALU.subtract,

@@ -24,9 +24,11 @@ PAIR = 2
 K_PASS = P * PACK
 BANK = 512
 HALVES = NODES // BANK
+BANK_TILES = BANK // P
 ROW_TILES = NODES // P
 NODE_PASSES = NODES // K_PASS
 NODE_TILES = NODE_PASSES * PACK
+STEPS = BATCH * ROW_TILES
 SCALE = 1.0 / math.sqrt(HEAD_DIM)
 MASKED = 1.0e30
 
@@ -42,8 +44,9 @@ def tile_gatlayer_pa_t_kernel(tc, q, k, h, w_v, adj, out):
     with ExitStack() as stack:
         const = stack.enter_context(tc.tile_pool(name="const", bufs=1))
         batch = stack.enter_context(tc.tile_pool(name="batch", bufs=2))
-        work = stack.enter_context(tc.tile_pool(name="work", bufs=3))
-        psum_s = stack.enter_context(tc.psum_pool(name="psum_s", bufs=5))
+        work = stack.enter_context(tc.tile_pool(name="work", bufs=4))
+        psum_0 = stack.enter_context(tc.psum_pool(name="psum_0", bufs=3))
+        psum_1 = stack.enter_context(tc.psum_pool(name="psum_1", bufs=2))
         psum_x = stack.enter_context(tc.psum_pool(name="psum_x", bufs=3))
 
         ident_bf16 = const.tile([P, P], BF16)
@@ -51,136 +54,289 @@ def tile_gatlayer_pa_t_kernel(tc, q, k, h, w_v, adj, out):
         ident_f32 = const.tile([P, P], F32)
         make_identity(nc, ident_f32[:])
 
+        mask_bias = const.tile([P, ROW_TILES, NODES], BF16)
+        mask_cols = const.tile([P, ROW_TILES, NODES // P, P], F32)
+        w_codes = const.tile([P, HEADS * HEAD_DIM], U32, align_bytes=64)
+        w_scales = const.tile([P, HEADS * HEAD_DIM], U8, align_bytes=64)
+
+        rows_of = {}
+        cols_of = {}
+        h_of = {}
+        v_of = {}
+        parked = {}
+        kept = {}
+
+        def in_range(s):
+            return 0 <= s < STEPS
+
+
         def load_batch(b):
+            if not 0 <= b < BATCH:
+                return
             q_rows = batch.tile([P, HEADS, ROW_TILES, HEAD_DIM], BF16)
             nc.sync.dma_start(out=q_rows[:], in_=q[b].rearrange("n (t p) d -> p n t d", p=P))
             k_rows = batch.tile([P, HEADS, ROW_TILES, HEAD_DIM], BF16)
             nc.sync.dma_start(out=k_rows[:], in_=k[b].rearrange("n (t p) d -> p n t d", p=P))
             h_rows = batch.tile([P, NODE_TILES // PAIR, PAIR, IN_DIM], BF16)
             nc.sync.dma_start(out=h_rows[:], in_=h[b].rearrange("(c p e) f -> p c e f", p=P, e=PAIR))
-            return q_rows, k_rows, h_rows
+            rows_of[b] = (q_rows, k_rows, h_rows)
 
-        def prepare_batch(q_rows, k_rows, h_rows):
-            q_cols = batch.tile([P, HEADS, NODES], BF16)
-            k_cols = batch.tile([P, HEADS, NODES], BF16)
-            for rows, cols in ((q_rows, q_cols), (k_rows, k_cols)):
-                for n in range(HEADS):
-                    flipped = psum_x.tile([P, ROW_TILES, P], BF16, name="flipped", tag="shared")
-                    for t in range(ROW_TILES):
-                        nc.tensor.transpose(flipped[:, t, :], rows[:, n, t, :], ident_bf16[:])
-                    nc.scalar.copy(out=cols[:, n, :], in_=flipped[:].rearrange("p t i -> p (t i)"))
-
-            h_words = h_rows[:].bitcast(F32)
-            h_grouped = batch.tile([P, NODE_TILES, P, PACK], BF16, align_bytes=64)
-            h_grouped_words = h_grouped[:].bitcast(F32)
-            for c in range(NODE_TILES // PAIR):
+        def prepare_on_tensor(b, part):
+            if not 0 <= b < BATCH:
+                return
+            if part == 0:
+                q_cols = batch.tile([P, HEADS, NODES], BF16)
+                k_cols = batch.tile([P, HEADS, NODES], BF16)
+                cols_of[b] = (q_cols, k_cols)
+                h_grouped = batch.tile([P, NODE_TILES, P, PACK], BF16, align_bytes=64)
+                h_codes = batch.tile([P, NODES], U32, align_bytes=64)
+                h_scales = batch.tile([P, NODES], U8, align_bytes=64)
+                h_of[b] = (h_grouped, h_codes, h_scales)
+            if part == NODE_TILES // PAIR:
+                v_grouped = batch.tile([P, NODE_PASSES * HEADS, HEAD_DIM, PACK], BF16, align_bytes=64)
+                v_codes = batch.tile([P, NODE_PASSES * HEADS * HEAD_DIM], U32, align_bytes=64)
+                v_scales = batch.tile([P, NODE_PASSES * HEADS * HEAD_DIM], U8, align_bytes=64)
+                v_of[b] = (v_grouped, v_codes, v_scales)
+            if part < NODE_TILES // PAIR:
+                h_words = rows_of[b][2][:].bitcast(F32)
                 h_flipped = psum_x.tile([P, PAIR, PAIR, P], F32, name="h_flipped", tag="shared")
                 for e in range(PAIR):
                     for u in range(PAIR):
-                        nc.tensor.transpose(h_flipped[:, e, u, :], h_words[:, c, e, block(u, P)], ident_f32[:])
-                nc.scalar.copy(
-                    out=h_grouped_words[:, block(c, PAIR), :, :],
-                    in_=h_flipped[:].rearrange("p e u r -> p e r u"),
-                )
-            h_codes = batch.tile([P, NODES], U32, align_bytes=64)
-            h_scales = batch.tile([P, NODES], U8, align_bytes=64)
-            nc.vector.quantize_mx(
-                out=h_codes[:].bitcast(FP8X4),
-                scales=h_scales[:],
-                in_=h_grouped[:].rearrange("p s r t -> p (s r t)"),
-            )
-
-            v_grouped = batch.tile([P, NODE_PASSES, HEADS, HEAD_DIM, PACK], BF16, align_bytes=64)
-            for g in range(NODE_PASSES):
-                for n in range(HEADS):
-                    v_sums = psum_x.tile([P, PACK, HEAD_DIM], F32, name="v_sums", tag="shared")
-                    for t in range(PACK):
-                        nc.tensor.matmul_mx(
-                            out=v_sums[:, t, :],
-                            lhsT=h_codes[:, block(PACK * g + t, P)].bitcast(FP8X4),
-                            lhsT_scale=h_scales[:, block(PACK * g + t, P)],
-                            rhs=w_codes[:, block(n, HEAD_DIM)].bitcast(FP8X4),
-                            rhs_scale=w_scales[:, block(n, HEAD_DIM)],
-                            start=True,
-                            stop=True,
-                        )
-                    nc.scalar.copy(out=v_grouped[:, g, n, :, :], in_=v_sums[:].rearrange("p t d -> p d t"))
-            v_codes = batch.tile([P, NODE_PASSES * HEADS * HEAD_DIM], U32, align_bytes=64)
-            v_scales = batch.tile([P, NODE_PASSES * HEADS * HEAD_DIM], U8, align_bytes=64)
-            nc.vector.quantize_mx(
-                out=v_codes[:].bitcast(FP8X4),
-                scales=v_scales[:],
-                in_=v_grouped[:].rearrange("p g n d t -> p (g n d t)"),
-            )
-            return q_cols, k_cols, v_codes, v_scales
-
-        def attend(b, it, q_cols, k_cols, v_codes, v_scales):
-            e_rows = work.tile([P, HEADS, NODES], BF16)
-            e_words = e_rows[:].bitcast(F32)
-            e_grouped = work.tile([P, HEADS, NODE_PASSES, P, PACK], BF16, align_bytes=64)
-            e_grouped_words = e_grouped[:].bitcast(F32)
-            part_sum = work.tile([P, HEADS, HALVES], F32)
-            for n in range(HEADS):
-                banks = []
-                part_max = work.tile([P, HALVES], F32)
-                for half in range(HALVES):
-                    s_sums = psum_s.tile([P, BANK], F32)
-                    nc.tensor.matmul(
-                        out=s_sums[:],
-                        lhsT=q_cols[:, n, block(it, P)],
-                        rhs=k_cols[:, n, block(half, BANK)],
+                        nc.tensor.transpose(h_flipped[:, e, u, :], h_words[:, part, e, block(u, P)], ident_f32[:])
+                parked["h", b] = h_flipped
+                n, which = divmod(part, 2)
+                qk_flipped = psum_x.tile([P, ROW_TILES, P], BF16, name="qk_flipped", tag="shared")
+                for t in range(ROW_TILES):
+                    nc.tensor.transpose(qk_flipped[:, t, :], rows_of[b][which][:, n, t, :], ident_bf16[:])
+                parked["qk", b] = qk_flipped
+            else:
+                g, n = divmod(part - NODE_TILES // PAIR, HEADS)
+                h_codes, h_scales = h_of[b][1], h_of[b][2]
+                v_sums = psum_x.tile([P, PACK, HEAD_DIM], F32, name="v_sums", tag="shared")
+                for t in range(PACK):
+                    nc.tensor.matmul_mx(
+                        out=v_sums[:, t, :],
+                        lhsT=h_codes[:, block(PACK * g + t, P)].bitcast(FP8X4),
+                        lhsT_scale=h_scales[:, block(PACK * g + t, P)],
+                        rhs=w_codes[:, block(n, HEAD_DIM)].bitcast(FP8X4),
+                        rhs_scale=w_scales[:, block(n, HEAD_DIM)],
                         start=True,
-                        stop=False,
+                        stop=True,
                     )
-                    for c in range(BANK // P):
-                        nc.tensor.matmul(
-                            out=s_sums[:, block(c, P)],
-                            lhsT=mask_cols[:, it, (BANK // P) * half + c, :],
-                            rhs=ident_f32[:],
-                            is_transpose=True,
-                            start=False,
-                            stop=(c == BANK // P - 1),
-                        )
-                    nc.vector.tensor_reduce(
-                        out=part_max[:, half : half + 1], in_=s_sums[:], axis=mybir.AxisListType.X, op=ALU.max
-                    )
-                    banks.append(s_sums)
-                neg_max = work.tile([P, 1], F32)
-                nc.vector.tensor_scalar(
-                    out=neg_max[:],
-                    in0=part_max[:, 0:1],
-                    scalar1=part_max[:, 1:2],
-                    scalar2=-SCALE,
-                    op0=ALU.max,
-                    op1=ALU.mult,
+                parked["v", b] = v_sums
+
+        def prepare_on_scalar(b, part):
+            if not 0 <= b < BATCH:
+                return
+            if part < NODE_TILES // PAIR:
+                nc.scalar.copy(
+                    out=h_of[b][0][:].bitcast(F32)[:, block(part, PAIR), :, :],
+                    in_=parked["h", b][:].rearrange("p e u r -> p e r u"),
                 )
-                for half in range(HALVES):
-                    nc.scalar.activation(
-                        out=e_rows[:, n, block(half, BANK)],
-                        in_=banks[half][:],
-                        func=FUNC.Exp,
-                        bias=neg_max[:],
-                        scale=SCALE,
-                        accum_out=part_sum[:, n, half : half + 1],
+            else:
+                nc.scalar.copy(
+                    out=v_of[b][0][:, part - NODE_TILES // PAIR, :, :],
+                    in_=parked["v", b][:].rearrange("p t d -> p d t"),
+                )
+
+        def prepare_on_vector(b, part):
+            if not 0 <= b < BATCH:
+                return
+            if part < NODE_TILES // PAIR:
+                n, which = divmod(part, 2)
+                nc.vector.tensor_copy(
+                    out=cols_of[b][which][:, n, :], in_=parked["qk", b][:].rearrange("p t i -> p (t i)")
+                )
+
+        def quantise_prepared(b, part):
+            if not 0 <= b < BATCH:
+                return
+            if part < NODE_TILES // PAIR:
+                grouped, codes, scales = h_of[b]
+                nc.vector.quantize_mx(
+                    out=codes[:, block(part, PAIR * P)].bitcast(FP8X4),
+                    scales=scales[:, block(part, PAIR * P)],
+                    in_=grouped[:, block(part, PAIR), :, :].rearrange("p s r t -> p (s r t)"),
+                )
+            else:
+                grouped, codes, scales = v_of[b]
+                nc.vector.quantize_mx(
+                    out=codes[:, block(part - NODE_TILES // PAIR, HEAD_DIM)].bitcast(FP8X4),
+                    scales=scales[:, block(part - NODE_TILES // PAIR, HEAD_DIM)],
+                    in_=grouped[:, part - NODE_TILES // PAIR, :, :].rearrange("p d t -> p (d t)"),
+                )
+
+        def build_mask(it):
+            nc.vector.tensor_scalar(
+                out=mask_bias[:, it, :],
+                in0=mask_bias[:, it, :],
+                scalar1=1.0,
+                scalar2=MASKED,
+                op0=ALU.subtract,
+                op1=ALU.mult,
+            )
+            mask_flipped = psum_x.tile([P, NODES // P, P], BF16, name="mask_flipped", tag="shared")
+            for c in range(NODES // P):
+                nc.tensor.transpose(mask_flipped[:, c, :], mask_bias[:, it, block(c, P)], ident_bf16[:])
+            nc.scalar.copy(out=mask_cols[:, it, :, :], in_=mask_flipped[:])
+
+
+        def scores_head0(s):
+            if not in_range(s):
+                return
+            b, it = divmod(s, ROW_TILES)
+            q_cols, k_cols = cols_of[b]
+            banks = []
+            for half in range(HALVES):
+                s_sums = psum_0.tile([P, BANK], F32, name="s_sums_0")
+                nc.tensor.matmul(
+                    out=s_sums[:],
+                    lhsT=q_cols[:, 0, block(it, P)],
+                    rhs=k_cols[:, 0, block(half, BANK)],
+                    start=True,
+                    stop=False,
+                )
+                for c in range(BANK_TILES):
+                    nc.tensor.matmul(
+                        out=s_sums[:, block(c, P)],
+                        lhsT=mask_cols[:, it, BANK_TILES * half + c, :],
+                        rhs=ident_f32[:],
+                        is_transpose=True,
+                        start=False,
+                        stop=(c == BANK_TILES - 1),
                     )
-                e_flipped = psum_x.tile([P, NODE_PASSES, PAIR, P], F32, name="e_flipped", tag="shared")
-                for g in range(NODE_PASSES):
-                    for u in range(PAIR):
-                        nc.tensor.transpose(e_flipped[:, g, u, :], e_words[:, n, block(PAIR * g + u, P)], ident_f32[:])
-                if n == 0:
-                    nc.scalar.copy(out=e_grouped_words[:, n], in_=e_flipped[:].rearrange("p g u i -> p g i u"))
-                else:
-                    nc.vector.tensor_copy(out=e_grouped_words[:, n], in_=e_flipped[:].rearrange("p g u i -> p g i u"))
+                banks.append(s_sums)
+            parked["s0", s] = banks
+
+        def scores_head1(s):
+            if not in_range(s):
+                return
+            b, it = divmod(s, ROW_TILES)
+            q_cols, k_cols = cols_of[b]
+            banks = []
+            for half in range(HALVES):
+                s_sums = psum_1.tile([P, BANK], F32, name="s_sums_1")
+                nc.tensor.matmul(
+                    out=s_sums[:],
+                    lhsT=q_cols[:, 1, block(it, P)],
+                    rhs=k_cols[:, 1, block(half, BANK)],
+                    start=True,
+                    stop=True,
+                )
+                banks.append(s_sums)
+            parked["s1", s] = banks
+
+        def max_head0(s):
+            if not in_range(s):
+                return
+            part_max = work.tile([P, HALVES], F32)
+            for half in range(HALVES):
+                nc.vector.tensor_reduce(
+                    out=part_max[:, half : half + 1], in_=parked["s0", s][half][:], axis=mybir.AxisListType.X, op=ALU.max
+                )
+            neg_max = work.tile([P, 1], F32, name="neg_max_0")
+            nc.vector.tensor_scalar(
+                out=neg_max[:],
+                in0=part_max[:, 0:1],
+                scalar1=part_max[:, 1:2],
+                scalar2=-SCALE,
+                op0=ALU.max,
+                op1=ALU.mult,
+            )
+            kept["neg_max_0", s] = neg_max
+
+        def exp_head0(s):
+            if not in_range(s):
+                return
+            e_rows = work.tile([P, NODES], BF16, name="e_rows_0")
+            part_sum = work.tile([P, HALVES], F32)
+            for half in range(HALVES):
+                nc.scalar.activation(
+                    out=e_rows[:, block(half, BANK)],
+                    in_=parked["s0", s][half][:],
+                    func=FUNC.Exp,
+                    bias=kept["neg_max_0", s][:],
+                    scale=SCALE,
+                    accum_out=part_sum[:, half : half + 1],
+                )
             row_sum = work.tile([P, HEADS], F32)
-            nc.vector.tensor_reduce(out=row_sum[:], in_=part_sum[:], axis=mybir.AxisListType.X, op=ALU.add)
+            nc.scalar.activation(out=row_sum[:, 0:1], in_=part_sum[:, 0:1], func=FUNC.Identity, bias=part_sum[:, 1:2])
+            kept["e_rows", s, 0] = e_rows
+            kept["row_sum", s] = row_sum
+
+        def mask_max_head1(s):
+            if not in_range(s):
+                return
+            it = s % ROW_TILES
+            scores = work.tile([P, NODES], F32)
+            for half in range(HALVES):
+                nc.vector.scalar_tensor_tensor(
+                    out=scores[:, block(half, BANK)],
+                    in0=parked["s1", s][half][:],
+                    scalar=SCALE,
+                    in1=mask_bias[:, it, block(half, BANK)],
+                    op0=ALU.mult,
+                    op1=ALU.add,
+                )
+            neg_max = work.tile([P, 1], F32, name="neg_max_1")
+            nc.vector.tensor_reduce(out=neg_max[:], in_=scores[:], axis=mybir.AxisListType.X, op=ALU.max, negate=True)
+            kept["scores", s] = scores
+            kept["neg_max_1", s] = neg_max
+
+        def exp_head1(s):
+            if not in_range(s):
+                return
+            e_rows = work.tile([P, NODES], BF16, name="e_rows_1")
+            nc.scalar.activation(
+                out=e_rows[:],
+                in_=kept["scores", s][:],
+                func=FUNC.Exp,
+                bias=kept["neg_max_1", s][:],
+                scale=1.0,
+                accum_out=kept["row_sum", s][:, 1:2],
+            )
+            kept["e_rows", s, 1] = e_rows
+
+        def flip(s, n):
+            if not in_range(s):
+                return
+            e_words = kept["e_rows", s, n][:].bitcast(F32)
+            e_flipped = psum_x.tile([P, NODE_PASSES, PAIR, P], F32, name="e_flipped", tag="shared")
+            for g in range(NODE_PASSES):
+                for u in range(PAIR):
+                    nc.tensor.transpose(e_flipped[:, g, u, :], e_words[:, block(PAIR * g + u, P)], ident_f32[:])
+            parked["e", s, n] = e_flipped
+
+        def copy_flipped(s):
+            if not in_range(s):
+                return
+            e_grouped = work.tile([P, HEADS, NODE_PASSES, P, PACK], BF16, align_bytes=64)
+            for n in range(HEADS):
+                nc.scalar.copy(
+                    out=e_grouped[:].bitcast(F32)[:, n], in_=parked["e", s, n][:].rearrange("p g u i -> p g i u")
+                )
+            kept["e_grouped", s] = e_grouped
+
+        def quantise_e(s):
+            if not in_range(s):
+                return
             e_codes = work.tile([P, HEADS * NODE_PASSES * P], U32, align_bytes=64)
             e_scales = work.tile([P, HEADS * NODE_PASSES * P], U8, align_bytes=64)
             nc.vector.quantize_mx(
                 out=e_codes[:].bitcast(FP8X4),
                 scales=e_scales[:],
-                in_=e_grouped[:].rearrange("p n g i t -> p (n g i t)"),
+                in_=kept["e_grouped", s][:].rearrange("p n g i t -> p (n g i t)"),
             )
+            inv_sum = work.tile([P, HEADS], F32)
+            nc.vector.reciprocal(out=inv_sum[:], in_=kept["row_sum", s][:])
+            kept["e_mx", s] = (e_codes, e_scales)
+            kept["inv_sum", s] = inv_sum
 
+        def multiply(s):
+            if not in_range(s):
+                return
+            e_codes, e_scales = kept["e_mx", s]
+            v_codes, v_scales = v_of[s // ROW_TILES][1], v_of[s // ROW_TILES][2]
             o_sums = psum_x.tile([P, HEADS, HEAD_DIM], F32, name="o_sums", tag="shared")
             for n in range(HEADS):
                 for g in range(NODE_PASSES):
@@ -193,14 +349,19 @@ def tile_gatlayer_pa_t_kernel(tc, q, k, h, w_v, adj, out):
                         start=(g == 0),
                         stop=(g == NODE_PASSES - 1),
                     )
-            inv_sum = work.tile([P, HEADS], F32)
-            nc.vector.reciprocal(out=inv_sum[:], in_=row_sum[:])
+            parked["o", s] = o_sums
+
+        def divide_and_store(s):
+            if not in_range(s):
+                return
+            b, it = divmod(s, ROW_TILES)
             o_rows = work.tile([P, HEADS, HEAD_DIM], F32)
             for n in range(HEADS):
-                nc.scalar.activation(out=o_rows[:, n, :], in_=o_sums[:, n, :], func=FUNC.Copy, scale=inv_sum[:, n : n + 1])
+                nc.scalar.activation(
+                    out=o_rows[:, n, :], in_=parked["o", s][:, n, :], func=FUNC.Copy, scale=kept["inv_sum", s][:, n : n + 1]
+                )
             nc.gpsimd.dma_start(out=out[b, block(it, P), :], in_=o_rows[:].rearrange("p n d -> p (n d)"))
 
-        loaded = load_batch(0)
 
         w_rows = const.tile([P, PACK, HEADS * HEAD_DIM], BF16)
         for u in range(PAIR):
@@ -210,34 +371,35 @@ def tile_gatlayer_pa_t_kernel(tc, q, k, h, w_v, adj, out):
             )
         w_grouped = const.tile([P, HEADS * HEAD_DIM, PACK], BF16, align_bytes=64)
         nc.vector.tensor_copy(out=w_grouped[:], in_=w_rows[:].rearrange("p t c -> p c t"))
-        w_codes = const.tile([P, HEADS * HEAD_DIM], U32, align_bytes=64)
-        w_scales = const.tile([P, HEADS * HEAD_DIM], U8, align_bytes=64)
         nc.vector.quantize_mx(
             out=w_codes[:].bitcast(FP8X4),
             scales=w_scales[:],
             in_=w_grouped[:].rearrange("p c t -> p (c t)"),
         )
 
-        adj_rows = const.tile([P, ROW_TILES, NODES], BF16)
-        mask_cols = const.tile([P, ROW_TILES, NODES // P, P], F32)
+        load_batch(0)
         for it in range(ROW_TILES):
-            nc.sync.dma_start(out=adj_rows[:, it, :], in_=adj[block(it, P), :])
-            adj_flipped = psum_x.tile([P, NODES // P, P], BF16, name="adj_flipped", tag="shared")
-            for c in range(NODES // P):
-                nc.tensor.transpose(adj_flipped[:, c, :], adj_rows[:, it, block(c, P)], ident_bf16[:])
-            nc.vector.tensor_scalar(
-                out=mask_cols[:, it, :, :],
-                in0=adj_flipped[:],
-                scalar1=1.0,
-                scalar2=MASKED,
-                op0=ALU.subtract,
-                op1=ALU.mult,
-            )
+            nc.sync.dma_start(out=mask_bias[:, it, :], in_=adj[block(it, P), :])
 
-        prepared = prepare_batch(*loaded)
-        for b in range(BATCH):
-            current = prepared
-            if b + 1 < BATCH:
-                prepared = prepare_batch(*load_batch(b + 1))
-            for it in range(ROW_TILES):
-                attend(b, it, *current)
+        for s in range(-ROW_TILES, STEPS + 3):
+            b, it = divmod(s, ROW_TILES)
+            if it == 0:
+                load_batch(b + 2)
+            max_head0(s)
+            exp_head1(s - 1)
+            exp_head0(s)
+            quantise_e(s - 2)
+            quantise_prepared((s - 1) // ROW_TILES + 1, (s - 1) % ROW_TILES)
+            multiply(s - 3)
+            prepare_on_tensor(b + 1, it)
+            flip(s - 1, 1)
+            scores_head0(s + 1)
+            flip(s, 0)
+            scores_head1(s + 1)
+            copy_flipped(s - 1)
+            divide_and_store(s - 3)
+            prepare_on_scalar(b + 1, it)
+            mask_max_head1(s)
+            prepare_on_vector(b + 1, it)
+            if s < 0:
+                build_mask(it)

@@ -52,7 +52,7 @@ def tile_gatlayer_pa_t_kernel(tc, q, k, h, w_v, adj, out):
         ident_bf16 = const.tile([P, P], BF16)
         make_identity(nc, ident_bf16[:])
         ident_f32 = const.tile([P, P], F32)
-        make_identity(nc, ident_f32[:])
+        nc.vector.tensor_copy(out=ident_f32[:], in_=ident_bf16[:])
 
         mask_bias = const.tile([P, ROW_TILES, NODES], BF16)
         mask_cols = const.tile([P, ROW_TILES, NODES // P, P], F32)
@@ -360,7 +360,7 @@ def tile_gatlayer_pa_t_kernel(tc, q, k, h, w_v, adj, out):
                 nc.scalar.activation(
                     out=o_rows[:, n, :], in_=parked["o", s][:, n, :], func=FUNC.Copy, scale=kept["inv_sum", s][:, n : n + 1]
                 )
-            nc.gpsimd.dma_start(out=out[b, block(it, P), :], in_=o_rows[:].rearrange("p n d -> p (n d)"))
+            nc.sync.dma_start(out=out[b, block(it, P), :], in_=o_rows[:].rearrange("p n d -> p (n d)"))
 
 
         w_rows = const.tile([P, PACK, HEADS * HEAD_DIM], BF16)

@@ -29,6 +29,7 @@ ROW_TILES = NODES // P
 NODE_PASSES = NODES // K_PASS
 NODE_TILES = NODE_PASSES * PACK
 STEPS = BATCH * ROW_TILES
+MASK_ROUNDS = 4
 SCALE = 1.0 / math.sqrt(HEAD_DIM)
 MASKED = 1.0e30
 
@@ -73,12 +74,12 @@ def tile_gatlayer_pa_t_kernel(tc, q, k, h, w_v, adj, out):
         def load_batch(b):
             if not 0 <= b < BATCH:
                 return
+            h_rows = batch.tile([P, NODE_TILES // PAIR, PAIR, IN_DIM], BF16)
+            nc.sync.dma_start(out=h_rows[:], in_=h[b].rearrange("(c p e) f -> p c e f", p=P, e=PAIR))
             q_rows = batch.tile([P, HEADS, ROW_TILES, HEAD_DIM], BF16)
             nc.sync.dma_start(out=q_rows[:], in_=q[b].rearrange("n (t p) d -> p n t d", p=P))
             k_rows = batch.tile([P, HEADS, ROW_TILES, HEAD_DIM], BF16)
             nc.sync.dma_start(out=k_rows[:], in_=k[b].rearrange("n (t p) d -> p n t d", p=P))
-            h_rows = batch.tile([P, NODE_TILES // PAIR, PAIR, IN_DIM], BF16)
-            nc.sync.dma_start(out=h_rows[:], in_=h[b].rearrange("(c p e) f -> p c e f", p=P, e=PAIR))
             rows_of[b] = (q_rows, k_rows, h_rows)
 
         def prepare_on_tensor(b, part):
@@ -196,16 +197,17 @@ def tile_gatlayer_pa_t_kernel(tc, q, k, h, w_v, adj, out):
                     start=True,
                     stop=False,
                 )
+                banks.append(s_sums)
+            for half in range(HALVES):
                 for c in range(BANK_TILES):
                     nc.tensor.matmul(
-                        out=s_sums[:, block(c, P)],
+                        out=banks[half][:, block(c, P)],
                         lhsT=mask_cols[:, it, BANK_TILES * half + c, :],
                         rhs=ident_f32[:],
                         is_transpose=True,
                         start=False,
                         stop=(c == BANK_TILES - 1),
                     )
-                banks.append(s_sums)
             parked["s0", s] = banks
 
         def scores_head1(s):
@@ -226,7 +228,7 @@ def tile_gatlayer_pa_t_kernel(tc, q, k, h, w_v, adj, out):
                 banks.append(s_sums)
             parked["s1", s] = banks
 
-        def max_head0(s):
+        def bank_max_head0(s):
             if not in_range(s):
                 return
             part_max = work.tile([P, HALVES], F32)
@@ -234,6 +236,12 @@ def tile_gatlayer_pa_t_kernel(tc, q, k, h, w_v, adj, out):
                 nc.vector.tensor_reduce(
                     out=part_max[:, half : half + 1], in_=parked["s0", s][half][:], axis=mybir.AxisListType.X, op=ALU.max
                 )
+            kept["part_max", s] = part_max
+
+        def row_max_head0(s):
+            if not in_range(s):
+                return
+            part_max = kept["part_max", s]
             neg_max = work.tile([P, 1], F32, name="neg_max_0")
             nc.vector.tensor_scalar(
                 out=neg_max[:],
@@ -259,12 +267,18 @@ def tile_gatlayer_pa_t_kernel(tc, q, k, h, w_v, adj, out):
                     scale=SCALE,
                     accum_out=part_sum[:, half : half + 1],
                 )
+            kept["e_rows", s, 0] = e_rows
+            kept["part_sum", s] = part_sum
+
+        def row_sum_head0(s):
+            if not in_range(s):
+                return
+            part_sum = kept["part_sum", s]
             row_sum = work.tile([P, HEADS], F32)
             nc.scalar.activation(out=row_sum[:, 0:1], in_=part_sum[:, 0:1], func=FUNC.Identity, bias=part_sum[:, 1:2])
-            kept["e_rows", s, 0] = e_rows
             kept["row_sum", s] = row_sum
 
-        def mask_max_head1(s):
+        def mask_head1(s):
             if not in_range(s):
                 return
             it = s % ROW_TILES
@@ -278,9 +292,15 @@ def tile_gatlayer_pa_t_kernel(tc, q, k, h, w_v, adj, out):
                     op0=ALU.mult,
                     op1=ALU.add,
                 )
-            neg_max = work.tile([P, 1], F32, name="neg_max_1")
-            nc.vector.tensor_reduce(out=neg_max[:], in_=scores[:], axis=mybir.AxisListType.X, op=ALU.max, negate=True)
             kept["scores", s] = scores
+
+        def row_max_head1(s):
+            if not in_range(s):
+                return
+            neg_max = work.tile([P, 1], F32, name="neg_max_1")
+            nc.vector.tensor_reduce(
+                out=neg_max[:], in_=kept["scores", s][:], axis=mybir.AxisListType.X, op=ALU.max, negate=True
+            )
             kept["neg_max_1", s] = neg_max
 
         def exp_head1(s):
@@ -385,11 +405,11 @@ def tile_gatlayer_pa_t_kernel(tc, q, k, h, w_v, adj, out):
             b, it = divmod(s, ROW_TILES)
             if it == 0:
                 load_batch(b + 2)
-            max_head0(s)
+            bank_max_head0(s)
+            quantise_prepared((s - 1) // ROW_TILES + 1, (s - 1) % ROW_TILES)
+            row_max_head0(s)
             exp_head1(s - 1)
             exp_head0(s)
-            quantise_e(s - 2)
-            quantise_prepared((s - 1) // ROW_TILES + 1, (s - 1) % ROW_TILES)
             multiply(s - 3)
             prepare_on_tensor(b + 1, it)
             flip(s - 1, 1)
@@ -397,9 +417,13 @@ def tile_gatlayer_pa_t_kernel(tc, q, k, h, w_v, adj, out):
             flip(s, 0)
             scores_head1(s + 1)
             copy_flipped(s - 1)
+            row_sum_head0(s)
             divide_and_store(s - 3)
             prepare_on_scalar(b + 1, it)
-            mask_max_head1(s)
+            mask_head1(s)
+            quantise_e(s - 2)
             prepare_on_vector(b + 1, it)
-            if s < 0:
-                build_mask(it)
+            row_max_head1(s)
+            if -MASK_ROUNDS <= s < 0:
+                for it_mask in range(ROW_TILES // MASK_ROUNDS):
+                    build_mask((s + MASK_ROUNDS) * (ROW_TILES // MASK_ROUNDS) + it_mask)

@@ -29,7 +29,7 @@ ROW_TILES = NODES // P
 NODE_PASSES = NODES // K_PASS
 NODE_TILES = NODE_PASSES * PACK
 STEPS = BATCH * ROW_TILES
-MASK_ROUNDS = 4
+MASK_AHEAD = 2
 SCALE = 1.0 / math.sqrt(HEAD_DIM)
 MASKED = 1.0e30
 
@@ -62,6 +62,7 @@ def tile_gatlayer_pa_t_kernel(tc, q, k, h, w_v, adj, out):
 
         rows_of = {}
         cols_of = {}
+        nodes_of = {}
         h_of = {}
         v_of = {}
         parked = {}
@@ -70,116 +71,138 @@ def tile_gatlayer_pa_t_kernel(tc, q, k, h, w_v, adj, out):
         def in_range(s):
             return 0 <= s < STEPS
 
+        def plain_mask(it, half):
+            return half == 1 and 1 <= it <= ROW_TILES // 2
+
 
         def load_batch(b):
             if not 0 <= b < BATCH:
                 return
+            q_rows = batch.tile([P, HEADS, ROW_TILES, HEAD_DIM], BF16)
+            k_rows = batch.tile([P, HEADS, ROW_TILES, HEAD_DIM], BF16)
+            for n in range(HEADS):
+                nc.sync.dma_start(out=q_rows[:, n], in_=q[b, n].rearrange("(t p) d -> p t d", p=P))
+                nc.sync.dma_start(out=k_rows[:, n], in_=k[b, n].rearrange("(t p) d -> p t d", p=P))
+            rows_of[b] = (q_rows, k_rows)
+
+        def load_nodes(b):
+            if not 0 <= b < BATCH:
+                return
             h_rows = batch.tile([P, NODE_TILES // PAIR, PAIR, IN_DIM], BF16)
             nc.sync.dma_start(out=h_rows[:], in_=h[b].rearrange("(c p e) f -> p c e f", p=P, e=PAIR))
-            q_rows = batch.tile([P, HEADS, ROW_TILES, HEAD_DIM], BF16)
-            nc.sync.dma_start(out=q_rows[:], in_=q[b].rearrange("n (t p) d -> p n t d", p=P))
-            k_rows = batch.tile([P, HEADS, ROW_TILES, HEAD_DIM], BF16)
-            nc.sync.dma_start(out=k_rows[:], in_=k[b].rearrange("n (t p) d -> p n t d", p=P))
-            rows_of[b] = (q_rows, k_rows, h_rows)
+            nodes_of[b] = h_rows
 
-        def prepare_on_tensor(b, part):
+        def flip_qk(b, part):
             if not 0 <= b < BATCH:
                 return
             if part == 0:
                 q_cols = batch.tile([P, HEADS, NODES], BF16)
                 k_cols = batch.tile([P, HEADS, NODES], BF16)
                 cols_of[b] = (q_cols, k_cols)
+            n, which = divmod(part, 2)
+            qk_flipped = psum_x.tile([P, ROW_TILES, P], BF16, name="qk_flipped", tag="shared")
+            for t in range(ROW_TILES):
+                nc.tensor.transpose(qk_flipped[:, t, :], rows_of[b][which][:, n, t, :], ident_bf16[:])
+            parked["qk", b] = qk_flipped
+
+        def copy_qk(b, part, on_vector=False):
+            if not 0 <= b < BATCH:
+                return
+            n, which = divmod(part, 2)
+            copy = nc.vector.tensor_copy if on_vector else nc.scalar.copy
+            copy(out=cols_of[b][which][:, n, :], in_=parked["qk", b][:].rearrange("p t i -> p (t i)"))
+
+        def flip_nodes(b, part):
+            if not 0 <= b < BATCH:
+                return
+            if part == 0:
                 h_grouped = batch.tile([P, NODE_TILES, P, PACK], BF16, align_bytes=64)
                 h_codes = batch.tile([P, NODES], U32, align_bytes=64)
                 h_scales = batch.tile([P, NODES], U8, align_bytes=64)
                 h_of[b] = (h_grouped, h_codes, h_scales)
-            if part == NODE_TILES // PAIR:
+            h_words = nodes_of[b][:].bitcast(F32)
+            h_flipped = psum_x.tile([P, PAIR, PAIR, P], F32, name="h_flipped", tag="shared")
+            for e in range(PAIR):
+                for u in range(PAIR):
+                    nc.tensor.transpose(h_flipped[:, e, u, :], h_words[:, part, e, block(u, P)], ident_f32[:])
+            parked["h", b] = h_flipped
+
+        def copy_nodes(b, part):
+            if not 0 <= b < BATCH:
+                return
+            nc.scalar.copy(
+                out=h_of[b][0][:].bitcast(F32)[:, block(part, PAIR), :, :],
+                in_=parked["h", b][:].rearrange("p e u r -> p e r u"),
+            )
+
+        def quantise_nodes(b, part):
+            if not 0 <= b < BATCH:
+                return
+            grouped, codes, scales = h_of[b]
+            nc.vector.quantize_mx(
+                out=codes[:, block(part, PAIR * P)].bitcast(FP8X4),
+                scales=scales[:, block(part, PAIR * P)],
+                in_=grouped[:, block(part, PAIR), :, :].rearrange("p s r t -> p (s r t)"),
+            )
+
+        def values_on_tensor(b, part):
+            if not 0 <= b < BATCH:
+                return
+            if part == 0:
                 v_grouped = batch.tile([P, NODE_PASSES * HEADS, HEAD_DIM, PACK], BF16, align_bytes=64)
                 v_codes = batch.tile([P, NODE_PASSES * HEADS * HEAD_DIM], U32, align_bytes=64)
                 v_scales = batch.tile([P, NODE_PASSES * HEADS * HEAD_DIM], U8, align_bytes=64)
                 v_of[b] = (v_grouped, v_codes, v_scales)
-            if part < NODE_TILES // PAIR:
-                h_words = rows_of[b][2][:].bitcast(F32)
-                h_flipped = psum_x.tile([P, PAIR, PAIR, P], F32, name="h_flipped", tag="shared")
-                for e in range(PAIR):
-                    for u in range(PAIR):
-                        nc.tensor.transpose(h_flipped[:, e, u, :], h_words[:, part, e, block(u, P)], ident_f32[:])
-                parked["h", b] = h_flipped
-                n, which = divmod(part, 2)
-                qk_flipped = psum_x.tile([P, ROW_TILES, P], BF16, name="qk_flipped", tag="shared")
-                for t in range(ROW_TILES):
-                    nc.tensor.transpose(qk_flipped[:, t, :], rows_of[b][which][:, n, t, :], ident_bf16[:])
-                parked["qk", b] = qk_flipped
-            else:
-                g, n = divmod(part - NODE_TILES // PAIR, HEADS)
-                h_codes, h_scales = h_of[b][1], h_of[b][2]
-                v_sums = psum_x.tile([P, PACK, HEAD_DIM], F32, name="v_sums", tag="shared")
-                for t in range(PACK):
-                    nc.tensor.matmul_mx(
-                        out=v_sums[:, t, :],
-                        lhsT=h_codes[:, block(PACK * g + t, P)].bitcast(FP8X4),
-                        lhsT_scale=h_scales[:, block(PACK * g + t, P)],
-                        rhs=w_codes[:, block(n, HEAD_DIM)].bitcast(FP8X4),
-                        rhs_scale=w_scales[:, block(n, HEAD_DIM)],
-                        start=True,
-                        stop=True,
-                    )
-                parked["v", b] = v_sums
+            g, n = divmod(part, HEADS)
+            h_codes, h_scales = h_of[b][1], h_of[b][2]
+            v_sums = psum_x.tile([P, PACK, HEAD_DIM], F32, name="v_sums", tag="shared")
+            for t in range(PACK):
+                nc.tensor.matmul_mx(
+                    out=v_sums[:, t, :],
+                    lhsT=h_codes[:, block(PACK * g + t, P)].bitcast(FP8X4),
+                    lhsT_scale=h_scales[:, block(PACK * g + t, P)],
+                    rhs=w_codes[:, block(n, HEAD_DIM)].bitcast(FP8X4),
+                    rhs_scale=w_scales[:, block(n, HEAD_DIM)],
+                    start=True,
+                    stop=True,
+                )
+            parked["v", b, part] = v_sums
 
-        def prepare_on_scalar(b, part):
+        def copy_values(b, part):
             if not 0 <= b < BATCH:
                 return
-            if part < NODE_TILES // PAIR:
-                nc.scalar.copy(
-                    out=h_of[b][0][:].bitcast(F32)[:, block(part, PAIR), :, :],
-                    in_=parked["h", b][:].rearrange("p e u r -> p e r u"),
-                )
-            else:
-                nc.scalar.copy(
-                    out=v_of[b][0][:, part - NODE_TILES // PAIR, :, :],
-                    in_=parked["v", b][:].rearrange("p t d -> p d t"),
-                )
+            nc.scalar.copy(out=v_of[b][0][:, part, :, :], in_=parked["v", b, part][:].rearrange("p t d -> p d t"))
 
-        def prepare_on_vector(b, part):
+        def quantise_values(b, part):
             if not 0 <= b < BATCH:
                 return
-            if part < NODE_TILES // PAIR:
-                n, which = divmod(part, 2)
-                nc.vector.tensor_copy(
-                    out=cols_of[b][which][:, n, :], in_=parked["qk", b][:].rearrange("p t i -> p (t i)")
-                )
+            grouped, codes, scales = v_of[b]
+            nc.vector.quantize_mx(
+                out=codes[:, block(part, HEAD_DIM)].bitcast(FP8X4),
+                scales=scales[:, block(part, HEAD_DIM)],
+                in_=grouped[:, part, :, :].rearrange("p d t -> p (d t)"),
+            )
 
-        def quantise_prepared(b, part):
-            if not 0 <= b < BATCH:
-                return
-            if part < NODE_TILES // PAIR:
-                grouped, codes, scales = h_of[b]
-                nc.vector.quantize_mx(
-                    out=codes[:, block(part, PAIR * P)].bitcast(FP8X4),
-                    scales=scales[:, block(part, PAIR * P)],
-                    in_=grouped[:, block(part, PAIR), :, :].rearrange("p s r t -> p (s r t)"),
-                )
-            else:
-                grouped, codes, scales = v_of[b]
-                nc.vector.quantize_mx(
-                    out=codes[:, block(part - NODE_TILES // PAIR, HEAD_DIM)].bitcast(FP8X4),
-                    scales=scales[:, block(part - NODE_TILES // PAIR, HEAD_DIM)],
-                    in_=grouped[:, part - NODE_TILES // PAIR, :, :].rearrange("p d t -> p (d t)"),
-                )
-
-        def build_mask(it):
-            nc.vector.tensor_scalar(
+        def bias_mask(engine, it):
+            engine.tensor_scalar(
                 out=mask_bias[:, it, :],
                 in0=mask_bias[:, it, :],
-                scalar1=1.0,
+                scalar1=-1.0,
                 scalar2=MASKED,
-                op0=ALU.subtract,
+                op0=ALU.add,
                 op1=ALU.mult,
             )
+
+        def flip_mask(it):
+            columns = BANK_TILES if plain_mask(it, 1) else NODES // P
             mask_flipped = psum_x.tile([P, NODES // P, P], BF16, name="mask_flipped", tag="shared")
-            for c in range(NODES // P):
+            for c in range(columns):
                 nc.tensor.transpose(mask_flipped[:, c, :], mask_bias[:, it, block(c, P)], ident_bf16[:])
-            nc.scalar.copy(out=mask_cols[:, it, :, :], in_=mask_flipped[:])
+            parked["mask", it] = mask_flipped[:, 0:columns, :]
+
+        def copy_mask(it):
+            flipped = parked["mask", it]
+            nc.scalar.copy(out=mask_cols[:, it, 0 : flipped.shape[1], :], in_=flipped)
 
 
         def scores_head0(s):
@@ -199,6 +222,15 @@ def tile_gatlayer_pa_t_kernel(tc, q, k, h, w_v, adj, out):
                 )
                 banks.append(s_sums)
             for half in range(HALVES):
+                if plain_mask(it, half):
+                    nc.tensor.matmul(
+                        out=banks[half][:],
+                        lhsT=ident_bf16[:],
+                        rhs=mask_bias[:, it, block(half, BANK)],
+                        start=False,
+                        stop=True,
+                    )
+                    continue
                 for c in range(BANK_TILES):
                     nc.tensor.matmul(
                         out=banks[half][:, block(c, P)],
@@ -275,7 +307,7 @@ def tile_gatlayer_pa_t_kernel(tc, q, k, h, w_v, adj, out):
                 return
             part_sum = kept["part_sum", s]
             row_sum = work.tile([P, HEADS], F32)
-            nc.scalar.activation(out=row_sum[:, 0:1], in_=part_sum[:, 0:1], func=FUNC.Identity, bias=part_sum[:, 1:2])
+            nc.gpsimd.tensor_tensor(out=row_sum[:, 0:1], in0=part_sum[:, 0:1], in1=part_sum[:, 1:2], op=ALU.add)
             kept["row_sum", s] = row_sum
 
         def mask_head1(s):
@@ -383,47 +415,87 @@ def tile_gatlayer_pa_t_kernel(tc, q, k, h, w_v, adj, out):
             nc.sync.dma_start(out=out[b, block(it, P), :], in_=o_rows[:].rearrange("p n d -> p (n d)"))
 
 
+        load_batch(0)
+        for it in range(MASK_AHEAD):
+            nc.sync.dma_start(out=mask_bias[:, it, :], in_=adj[block(it, P), :])
+        load_nodes(0)
         w_rows = const.tile([P, PACK, HEADS * HEAD_DIM], BF16)
         for u in range(PAIR):
             nc.sync.dma_start(
                 out=w_rows[:, block(u, PAIR), :],
                 in_=w_v[block(u, PAIR * P), :].rearrange("(p e) c -> p e c", e=PAIR),
             )
+        for it in range(MASK_AHEAD, ROW_TILES):
+            nc.sync.dma_start(out=mask_bias[:, it, :], in_=adj[block(it, P), :])
+        load_batch(1)
+        load_nodes(1)
+
+        for part in range(2 * HEADS):
+            flip_qk(0, part)
+            copy_qk(0, part, on_vector=(part % 2 == 0))
+        for it in range(ROW_TILES):
+            bias_mask(nc.vector if it < MASK_AHEAD else nc.gpsimd, it)
+        for it in range(MASK_AHEAD):
+            flip_mask(it)
+            copy_mask(it)
+        for part in range(NODE_TILES // PAIR):
+            flip_nodes(0, part)
+            copy_nodes(0, part)
         w_grouped = const.tile([P, HEADS * HEAD_DIM, PACK], BF16, align_bytes=64)
         nc.vector.tensor_copy(out=w_grouped[:], in_=w_rows[:].rearrange("p t c -> p c t"))
+        for part in range(NODE_TILES // PAIR):
+            quantise_nodes(0, part)
         nc.vector.quantize_mx(
             out=w_codes[:].bitcast(FP8X4),
             scales=w_scales[:],
             in_=w_grouped[:].rearrange("p c t -> p (c t)"),
         )
 
-        load_batch(0)
-        for it in range(ROW_TILES):
-            nc.sync.dma_start(out=mask_bias[:, it, :], in_=adj[block(it, P), :])
-
-        for s in range(-ROW_TILES, STEPS + 3):
+        half_batch = ROW_TILES // 2
+        for s in range(-1, STEPS + 3):
             b, it = divmod(s, ROW_TILES)
             if it == 0:
                 load_batch(b + 2)
+                load_nodes(b + 2)
+            rows_part = (b + 1, it) if s >= 0 and it < half_batch else (BATCH, 0)
+            values_parts = [(b + 1, it - half_batch)] if s >= 0 and it >= half_batch else []
+            if s + 1 < half_batch:
+                values_parts.append((0, s + 1))
+            b_before, it_before = divmod(s - 1, ROW_TILES)
+            if s >= 1 and it_before < half_batch:
+                quantise_before = [(quantise_nodes, b_before + 1, it_before)]
+            elif s >= 1:
+                quantise_before = [(quantise_values, b_before + 1, it_before - half_batch)]
+            else:
+                quantise_before = []
+            if 0 <= s < half_batch:
+                quantise_before.append((quantise_values, 0, s))
+
             bank_max_head0(s)
-            quantise_prepared((s - 1) // ROW_TILES + 1, (s - 1) % ROW_TILES)
+            for quantise, b_part, part in quantise_before:
+                quantise(b_part, part)
             row_max_head0(s)
             exp_head1(s - 1)
             exp_head0(s)
-            multiply(s - 3)
-            prepare_on_tensor(b + 1, it)
             flip(s - 1, 1)
             scores_head0(s + 1)
             flip(s, 0)
             scores_head1(s + 1)
+            multiply(s - 3)
+            for b_part, part in values_parts:
+                values_on_tensor(b_part, part)
+            flip_nodes(*rows_part)
+            flip_qk(*rows_part)
             copy_flipped(s - 1)
             row_sum_head0(s)
             divide_and_store(s - 3)
-            prepare_on_scalar(b + 1, it)
+            copy_nodes(*rows_part)
+            for b_part, part in values_parts:
+                copy_values(b_part, part)
             mask_head1(s)
             quantise_e(s - 2)
-            prepare_on_vector(b + 1, it)
+            copy_qk(*rows_part, on_vector=(it != 3))
             row_max_head1(s)
-            if -MASK_ROUNDS <= s < 0:
-                for it_mask in range(ROW_TILES // MASK_ROUNDS):
-                    build_mask((s + MASK_ROUNDS) * (ROW_TILES // MASK_ROUNDS) + it_mask)
+            if 0 <= s < ROW_TILES - MASK_AHEAD:
+                flip_mask(s + MASK_AHEAD)
+                copy_mask(s + MASK_AHEAD)

import math
from contextlib import ExitStack

import concourse.mybir as mybir
from concourse.masks import make_identity

F32 = mybir.dt.float32
BF16 = mybir.dt.bfloat16
U32 = mybir.dt.uint32
U8 = mybir.dt.uint8
FP8X4 = mybir.dt.float8_e4m3fn_x4
ALU = mybir.AluOpType
FUNC = mybir.ActivationFunctionType

BATCH = 8
HEADS = 2
NODES = 1024
HEAD_DIM = 128
IN_DIM = 512

P = 128
PACK = 4
PAIR = 2
K_PASS = P * PACK
BANK = 512
HALVES = NODES // BANK
BANK_TILES = BANK // P
ROW_TILES = NODES // P
NODE_PASSES = NODES // K_PASS
NODE_TILES = NODE_PASSES * PACK
STEPS = BATCH * ROW_TILES
MASK_AHEAD = 2
SCALE = 1.0 / math.sqrt(HEAD_DIM)
MASKED = 1.0e30

FLOPS = 2 * BATCH * NODES * IN_DIM * HEADS * HEAD_DIM + 2 * 2 * BATCH * HEADS * NODES * NODES * HEAD_DIM


def block(index, width):
    return slice(index * width, (index + 1) * width)


def tile_gatlayer_pa_t_kernel(tc, q, k, h, w_v, adj, out):
    nc = tc.nc
    with ExitStack() as stack:
        const = stack.enter_context(tc.tile_pool(name="const", bufs=1))
        batch = stack.enter_context(tc.tile_pool(name="batch", bufs=2))
        work = stack.enter_context(tc.tile_pool(name="work", bufs=4))
        psum_0 = stack.enter_context(tc.psum_pool(name="psum_0", bufs=3))
        psum_1 = stack.enter_context(tc.psum_pool(name="psum_1", bufs=2))
        psum_x = stack.enter_context(tc.psum_pool(name="psum_x", bufs=3))

        ident_bf16 = const.tile([P, P], BF16)
        make_identity(nc, ident_bf16[:])
        ident_f32 = const.tile([P, P], F32)
        nc.vector.tensor_copy(out=ident_f32[:], in_=ident_bf16[:])

        mask_bias = const.tile([P, ROW_TILES, NODES], BF16)
        mask_cols = const.tile([P, ROW_TILES, NODES // P, P], F32)
        w_codes = const.tile([P, HEADS * HEAD_DIM], U32, align_bytes=64)
        w_scales = const.tile([P, HEADS * HEAD_DIM], U8, align_bytes=64)

        rows_of = {}
        cols_of = {}
        nodes_of = {}
        h_of = {}
        v_of = {}
        parked = {}
        kept = {}

        def in_range(s):
            return 0 <= s < STEPS

        def plain_mask(it, half):
            return half == 1 and 1 <= it <= ROW_TILES // 2


        def load_batch(b):
            if not 0 <= b < BATCH:
                return
            q_rows = batch.tile([P, HEADS, ROW_TILES, HEAD_DIM], BF16)
            k_rows = batch.tile([P, HEADS, ROW_TILES, HEAD_DIM], BF16)
            for n in range(HEADS):
                nc.sync.dma_start(out=q_rows[:, n], in_=q[b, n].rearrange("(t p) d -> p t d", p=P))
                nc.sync.dma_start(out=k_rows[:, n], in_=k[b, n].rearrange("(t p) d -> p t d", p=P))
            rows_of[b] = (q_rows, k_rows)

        def load_nodes(b):
            if not 0 <= b < BATCH:
                return
            h_rows = batch.tile([P, NODE_TILES // PAIR, PAIR, IN_DIM], BF16)
            nc.sync.dma_start(out=h_rows[:], in_=h[b].rearrange("(c p e) f -> p c e f", p=P, e=PAIR))
            nodes_of[b] = h_rows

        def flip_qk(b, part):
            if not 0 <= b < BATCH:
                return
            if part == 0:
                q_cols = batch.tile([P, HEADS, NODES], BF16)
                k_cols = batch.tile([P, HEADS, NODES], BF16)
                cols_of[b] = (q_cols, k_cols)
            n, which = divmod(part, 2)
            qk_flipped = psum_x.tile([P, ROW_TILES, P], BF16, name="qk_flipped", tag="shared")
            for t in range(ROW_TILES):
                nc.tensor.transpose(qk_flipped[:, t, :], rows_of[b][which][:, n, t, :], ident_bf16[:])
            parked["qk", b] = qk_flipped

        def copy_qk(b, part, on_vector=False):
            if not 0 <= b < BATCH:
                return
            n, which = divmod(part, 2)
            copy = nc.vector.tensor_copy if on_vector else nc.scalar.copy
            copy(out=cols_of[b][which][:, n, :], in_=parked["qk", b][:].rearrange("p t i -> p (t i)"))

        def flip_nodes(b, part):
            if not 0 <= b < BATCH:
                return
            if part == 0:
                h_grouped = batch.tile([P, NODE_TILES, P, PACK], BF16, align_bytes=64)
                h_codes = batch.tile([P, NODES], U32, align_bytes=64)
                h_scales = batch.tile([P, NODES], U8, align_bytes=64)
                h_of[b] = (h_grouped, h_codes, h_scales)
            h_words = nodes_of[b][:].bitcast(F32)
            h_flipped = psum_x.tile([P, PAIR, PAIR, P], F32, name="h_flipped", tag="shared")
            for e in range(PAIR):
                for u in range(PAIR):
                    nc.tensor.transpose(h_flipped[:, e, u, :], h_words[:, part, e, block(u, P)], ident_f32[:])
            parked["h", b] = h_flipped

        def copy_nodes(b, part):
            if not 0 <= b < BATCH:
                return
            nc.scalar.copy(
                out=h_of[b][0][:].bitcast(F32)[:, block(part, PAIR), :, :],
                in_=parked["h", b][:].rearrange("p e u r -> p e r u"),
            )

        def quantise_nodes(b, part):
            if not 0 <= b < BATCH:
                return
            grouped, codes, scales = h_of[b]
            nc.vector.quantize_mx(
                out=codes[:, block(part, PAIR * P)].bitcast(FP8X4),
                scales=scales[:, block(part, PAIR * P)],
                in_=grouped[:, block(part, PAIR), :, :].rearrange("p s r t -> p (s r t)"),
            )

        def values_on_tensor(b, part):
            if not 0 <= b < BATCH:
                return
            if part == 0:
                v_grouped = batch.tile([P, NODE_PASSES * HEADS, HEAD_DIM, PACK], BF16, align_bytes=64)
                v_codes = batch.tile([P, NODE_PASSES * HEADS * HEAD_DIM], U32, align_bytes=64)
                v_scales = batch.tile([P, NODE_PASSES * HEADS * HEAD_DIM], U8, align_bytes=64)
                v_of[b] = (v_grouped, v_codes, v_scales)
            g, n = divmod(part, HEADS)
            h_codes, h_scales = h_of[b][1], h_of[b][2]
            v_sums = psum_x.tile([P, PACK, HEAD_DIM], F32, name="v_sums", tag="shared")
            for t in range(PACK):
                nc.tensor.matmul_mx(
                    out=v_sums[:, t, :],
                    lhsT=h_codes[:, block(PACK * g + t, P)].bitcast(FP8X4),
                    lhsT_scale=h_scales[:, block(PACK * g + t, P)],
                    rhs=w_codes[:, block(n, HEAD_DIM)].bitcast(FP8X4),
                    rhs_scale=w_scales[:, block(n, HEAD_DIM)],
                    start=True,
                    stop=True,
                )
            parked["v", b, part] = v_sums

        def copy_values(b, part):
            if not 0 <= b < BATCH:
                return
            nc.scalar.copy(out=v_of[b][0][:, part, :, :], in_=parked["v", b, part][:].rearrange("p t d -> p d t"))

        def quantise_values(b, part):
            if not 0 <= b < BATCH:
                return
            grouped, codes, scales = v_of[b]
            nc.vector.quantize_mx(
                out=codes[:, block(part, HEAD_DIM)].bitcast(FP8X4),
                scales=scales[:, block(part, HEAD_DIM)],
                in_=grouped[:, part, :, :].rearrange("p d t -> p (d t)"),
            )

        def bias_mask(engine, it):
            engine.tensor_scalar(
                out=mask_bias[:, it, :],
                in0=mask_bias[:, it, :],
                scalar1=-1.0,
                scalar2=MASKED,
                op0=ALU.add,
                op1=ALU.mult,
            )

        def flip_mask(it):
            columns = BANK_TILES if plain_mask(it, 1) else NODES // P
            mask_flipped = psum_x.tile([P, NODES // P, P], BF16, name="mask_flipped", tag="shared")
            for c in range(columns):
                nc.tensor.transpose(mask_flipped[:, c, :], mask_bias[:, it, block(c, P)], ident_bf16[:])
            parked["mask", it] = mask_flipped[:, 0:columns, :]

        def copy_mask(it):
            flipped = parked["mask", it]
            nc.scalar.copy(out=mask_cols[:, it, 0 : flipped.shape[1], :], in_=flipped)


        def scores_head0(s):
            if not in_range(s):
                return
            b, it = divmod(s, ROW_TILES)
            q_cols, k_cols = cols_of[b]
            banks = []
            for half in range(HALVES):
                s_sums = psum_0.tile([P, BANK], F32, name="s_sums_0")
                nc.tensor.matmul(
                    out=s_sums[:],
                    lhsT=q_cols[:, 0, block(it, P)],
                    rhs=k_cols[:, 0, block(half, BANK)],
                    start=True,
                    stop=False,
                )
                banks.append(s_sums)
            for half in range(HALVES):
                if plain_mask(it, half):
                    nc.tensor.matmul(
                        out=banks[half][:],
                        lhsT=ident_bf16[:],
                        rhs=mask_bias[:, it, block(half, BANK)],
                        start=False,
                        stop=True,
                    )
                    continue
                for c in range(BANK_TILES):
                    nc.tensor.matmul(
                        out=banks[half][:, block(c, P)],
                        lhsT=mask_cols[:, it, BANK_TILES * half + c, :],
                        rhs=ident_f32[:],
                        is_transpose=True,
                        start=False,
                        stop=(c == BANK_TILES - 1),
                    )
            parked["s0", s] = banks

        def scores_head1(s):
            if not in_range(s):
                return
            b, it = divmod(s, ROW_TILES)
            q_cols, k_cols = cols_of[b]
            banks = []
            for half in range(HALVES):
                s_sums = psum_1.tile([P, BANK], F32, name="s_sums_1")
                nc.tensor.matmul(
                    out=s_sums[:],
                    lhsT=q_cols[:, 1, block(it, P)],
                    rhs=k_cols[:, 1, block(half, BANK)],
                    start=True,
                    stop=True,
                )
                banks.append(s_sums)
            parked["s1", s] = banks

        def bank_max_head0(s):
            if not in_range(s):
                return
            part_max = work.tile([P, HALVES], F32)
            for half in range(HALVES):
                nc.vector.tensor_reduce(
                    out=part_max[:, half : half + 1], in_=parked["s0", s][half][:], axis=mybir.AxisListType.X, op=ALU.max
                )
            kept["part_max", s] = part_max

        def row_max_head0(s):
            if not in_range(s):
                return
            part_max = kept["part_max", s]
            neg_max = work.tile([P, 1], F32, name="neg_max_0")
            nc.vector.tensor_scalar(
                out=neg_max[:],
                in0=part_max[:, 0:1],
                scalar1=part_max[:, 1:2],
                scalar2=-SCALE,
                op0=ALU.max,
                op1=ALU.mult,
            )
            kept["neg_max_0", s] = neg_max

        def exp_head0(s):
            if not in_range(s):
                return
            e_rows = work.tile([P, NODES], BF16, name="e_rows_0")
            part_sum = work.tile([P, HALVES], F32)
            for half in range(HALVES):
                nc.scalar.activation(
                    out=e_rows[:, block(half, BANK)],
                    in_=parked["s0", s][half][:],
                    func=FUNC.Exp,
                    bias=kept["neg_max_0", s][:],
                    scale=SCALE,
                    accum_out=part_sum[:, half : half + 1],
                )
            kept["e_rows", s, 0] = e_rows
            kept["part_sum", s] = part_sum

        def row_sum_head0(s):
            if not in_range(s):
                return
            part_sum = kept["part_sum", s]
            row_sum = work.tile([P, HEADS], F32)
            nc.gpsimd.tensor_tensor(out=row_sum[:, 0:1], in0=part_sum[:, 0:1], in1=part_sum[:, 1:2], op=ALU.add)
            kept["row_sum", s] = row_sum

        def mask_head1(s):
            if not in_range(s):
                return
            it = s % ROW_TILES
            scores = work.tile([P, NODES], F32)
            for half in range(HALVES):
                nc.vector.scalar_tensor_tensor(
                    out=scores[:, block(half, BANK)],
                    in0=parked["s1", s][half][:],
                    scalar=SCALE,
                    in1=mask_bias[:, it, block(half, BANK)],
                    op0=ALU.mult,
                    op1=ALU.add,
                )
            kept["scores", s] = scores

        def row_max_head1(s):
            if not in_range(s):
                return
            neg_max = work.tile([P, 1], F32, name="neg_max_1")
            nc.vector.tensor_reduce(
                out=neg_max[:], in_=kept["scores", s][:], axis=mybir.AxisListType.X, op=ALU.max, negate=True
            )
            kept["neg_max_1", s] = neg_max

        def exp_head1(s):
            if not in_range(s):
                return
            e_rows = work.tile([P, NODES], BF16, name="e_rows_1")
            nc.scalar.activation(
                out=e_rows[:],
                in_=kept["scores", s][:],
                func=FUNC.Exp,
                bias=kept["neg_max_1", s][:],
                scale=1.0,
                accum_out=kept["row_sum", s][:, 1:2],
            )
            kept["e_rows", s, 1] = e_rows

        def flip(s, n):
            if not in_range(s):
                return
            e_words = kept["e_rows", s, n][:].bitcast(F32)
            e_flipped = psum_x.tile([P, NODE_PASSES, PAIR, P], F32, name="e_flipped", tag="shared")
            for g in range(NODE_PASSES):
                for u in range(PAIR):
                    nc.tensor.transpose(e_flipped[:, g, u, :], e_words[:, block(PAIR * g + u, P)], ident_f32[:])
            parked["e", s, n] = e_flipped

        def copy_flipped(s):
            if not in_range(s):
                return
            e_grouped = work.tile([P, HEADS, NODE_PASSES, P, PACK], BF16, align_bytes=64)
            for n in range(HEADS):
                nc.scalar.copy(
                    out=e_grouped[:].bitcast(F32)[:, n], in_=parked["e", s, n][:].rearrange("p g u i -> p g i u")
                )
            kept["e_grouped", s] = e_grouped

        def quantise_e(s):
            if not in_range(s):
                return
            e_codes = work.tile([P, HEADS * NODE_PASSES * P], U32, align_bytes=64)
            e_scales = work.tile([P, HEADS * NODE_PASSES * P], U8, align_bytes=64)
            nc.vector.quantize_mx(
                out=e_codes[:].bitcast(FP8X4),
                scales=e_scales[:],
                in_=kept["e_grouped", s][:].rearrange("p n g i t -> p (n g i t)"),
            )
            inv_sum = work.tile([P, HEADS], F32)
            nc.vector.reciprocal(out=inv_sum[:], in_=kept["row_sum", s][:])
            kept["e_mx", s] = (e_codes, e_scales)
            kept["inv_sum", s] = inv_sum

        def multiply(s):
            if not in_range(s):
                return
            e_codes, e_scales = kept["e_mx", s]
            v_codes, v_scales = v_of[s // ROW_TILES][1], v_of[s // ROW_TILES][2]
            o_sums = psum_x.tile([P, HEADS, HEAD_DIM], F32, name="o_sums", tag="shared")
            for n in range(HEADS):
                for g in range(NODE_PASSES):
                    nc.tensor.matmul_mx(
                        out=o_sums[:, n, :],
                        lhsT=e_codes[:, block(NODE_PASSES * n + g, P)].bitcast(FP8X4),
                        lhsT_scale=e_scales[:, block(NODE_PASSES * n + g, P)],
                        rhs=v_codes[:, block(HEADS * g + n, HEAD_DIM)].bitcast(FP8X4),
                        rhs_scale=v_scales[:, block(HEADS * g + n, HEAD_DIM)],
                        start=(g == 0),
                        stop=(g == NODE_PASSES - 1),
                    )
            parked["o", s] = o_sums

        def divide_and_store(s):
            if not in_range(s):
                return
            b, it = divmod(s, ROW_TILES)
            o_rows = work.tile([P, HEADS, HEAD_DIM], F32)
            for n in range(HEADS):
                nc.scalar.activation(
                    out=o_rows[:, n, :], in_=parked["o", s][:, n, :], func=FUNC.Copy, scale=kept["inv_sum", s][:, n : n + 1]
                )
            nc.sync.dma_start(out=out[b, block(it, P), :], in_=o_rows[:].rearrange("p n d -> p (n d)"))


        load_batch(0)
        for it in range(MASK_AHEAD):
            nc.sync.dma_start(out=mask_bias[:, it, :], in_=adj[block(it, P), :])
        load_nodes(0)
        w_rows = const.tile([P, PACK, HEADS * HEAD_DIM], BF16)
        for u in range(PAIR):
            nc.sync.dma_start(
                out=w_rows[:, block(u, PAIR), :],
                in_=w_v[block(u, PAIR * P), :].rearrange("(p e) c -> p e c", e=PAIR),
            )
        for it in range(MASK_AHEAD, ROW_TILES):
            nc.sync.dma_start(out=mask_bias[:, it, :], in_=adj[block(it, P), :])
        load_batch(1)
        load_nodes(1)

        for part in range(2 * HEADS):
            flip_qk(0, part)
            copy_qk(0, part, on_vector=(part % 2 == 0))
        for it in range(ROW_TILES):
            bias_mask(nc.vector if it < MASK_AHEAD else nc.gpsimd, it)
        for it in range(MASK_AHEAD):
            flip_mask(it)
            copy_mask(it)
        for part in range(NODE_TILES // PAIR):
            flip_nodes(0, part)
            copy_nodes(0, part)
        w_grouped = const.tile([P, HEADS * HEAD_DIM, PACK], BF16, align_bytes=64)
        nc.vector.tensor_copy(out=w_grouped[:], in_=w_rows[:].rearrange("p t c -> p c t"))
        for part in range(NODE_TILES // PAIR):
            quantise_nodes(0, part)
        nc.vector.quantize_mx(
            out=w_codes[:].bitcast(FP8X4),
            scales=w_scales[:],
            in_=w_grouped[:].rearrange("p c t -> p (c t)"),
        )

        half_batch = ROW_TILES // 2
        for s in range(-1, STEPS + 3):
            b, it = divmod(s, ROW_TILES)
            if it == 0:
                load_batch(b + 2)
                load_nodes(b + 2)
            rows_part = (b + 1, it) if s >= 0 and it < half_batch else (BATCH, 0)
            values_parts = [(b + 1, it - half_batch)] if s >= 0 and it >= half_batch else []
            if s + 1 < half_batch:
                values_parts.append((0, s + 1))
            b_before, it_before = divmod(s - 1, ROW_TILES)
            if s >= 1 and it_before < half_batch:
                quantise_before = [(quantise_nodes, b_before + 1, it_before)]
            elif s >= 1:
                quantise_before = [(quantise_values, b_before + 1, it_before - half_batch)]
            else:
                quantise_before = []
            if 0 <= s < half_batch:
                quantise_before.append((quantise_values, 0, s))

            bank_max_head0(s)
            for quantise, b_part, part in quantise_before:
                quantise(b_part, part)
            row_max_head0(s)
            exp_head1(s - 1)
            exp_head0(s)
            flip(s - 1, 1)
            scores_head0(s + 1)
            flip(s, 0)
            scores_head1(s + 1)
            multiply(s - 3)
            for b_part, part in values_parts:
                values_on_tensor(b_part, part)
            flip_nodes(*rows_part)
            flip_qk(*rows_part)
            copy_flipped(s - 1)
            row_sum_head0(s)
            divide_and_store(s - 3)
            copy_nodes(*rows_part)
            for b_part, part in values_parts:
                copy_values(b_part, part)
            mask_head1(s)
            quantise_e(s - 2)
            copy_qk(*rows_part, on_vector=(it != 3))
            row_max_head1(s)
            if 0 <= s < ROW_TILES - MASK_AHEAD:
                flip_mask(s + MASK_AHEAD)
                copy_mask(s + MASK_AHEAD)
